import numpy as np
import ml_dtypes


def mxq(x, axis, fmt="e4m3"):
    dtype, down = {"e4m3": (ml_dtypes.float8_e4m3fn, 7), "e5m2": (ml_dtypes.float8_e5m2, 14)}[fmt]
    v = np.moveaxis(np.asarray(x, np.float32).astype(ml_dtypes.bfloat16).astype(np.float64), axis, -1)
    blocks = v.reshape(v.shape[:-1] + (-1, 32))
    amax = np.abs(blocks).max(-1, keepdims=True)
    byte = np.maximum(np.where(amax > 0, np.frexp(amax)[1] - 1 + 127, 0) - down, 1)
    scale = np.exp2(byte - 127.0)
    codes = (blocks / scale).astype(np.float32).astype(dtype).astype(np.float64)
    return np.moveaxis((codes * scale).reshape(v.shape), -1, axis)


WIDE = False


def mx_kscale(k):
    if not WIDE:
        return np.ones(k)
    levels = np.array([10, -10, 5, -5, 0])
    if k % 512:
        return np.exp2(np.random.permutation(np.resize(levels, k // 32))).repeat(32)
    a = np.empty((k // 512, 16))
    for p in range(k // 512):
        a[p, :8] = np.random.permutation(np.resize(levels, 8))
        for g in range(8):
            far = levels[np.abs(levels - a[p, g]) >= 10]
            a[p, g + 8] = far[np.random.randint(len(far))]
    return np.exp2(a.ravel()).repeat(32)


BF16 = ml_dtypes.bfloat16


def bf(x):
    return np.asarray(x, np.float32).astype(BF16)


def f64(x):
    return np.asarray(x).astype(np.float64)


B, H, S, D = 1, 2, 2048, 256
D2 = D // 2
LAMBDA_INIT = 0.8
EPS = 1e-5


def softmax(v):
    e = np.exp(v - v.max(-1, keepdims=True))
    return e / e.sum(-1, keepdims=True)


def setup_inputs():
    s = mx_kscale(S)
    c = np.log(2.0) * np.sqrt(D2)
    q = np.random.standard_normal((B, H, S, D))
    k = np.random.standard_normal((B, H, S, D))
    q[..., 0] = c
    q[..., D2] = c
    k[..., 0] += np.log2(s)
    k[..., D2] += np.log2(s)
    v = np.random.standard_normal((B, H, S, D)) * 0.005 * np.sqrt(S) / s[:, None] * s.mean()
    return {"query": bf(q), "key": bf(k), "value": bf(v),
            "lambda_params": bf(0.3 + 0.5 * np.random.random(H))}


def reference(query, key, value, lambda_params):
    query, key, value, lambda_params = f64(query), f64(key), f64(value), f64(lambda_params)
    scale = 1.0 / np.sqrt(D2)
    q1, q2 = query[..., :D2], query[..., D2:]
    k1, k2 = key[..., :D2], key[..., D2:]
    a1 = softmax(q1 @ k1.transpose(0, 1, 3, 2) * scale)
    a2 = softmax(q2 @ k2.transpose(0, 1, 3, 2) * scale)
    lam = lambda_params[None, :, None, None]
    attn = a1 - lam * a2
    out = mxq(attn, 3, "e4m3") @ mxq(value, 2, "e4m3")
    mean = out.mean(-1, keepdims=True)
    var = ((out - mean) ** 2).mean(-1, keepdims=True)
    out = (out - mean) / np.sqrt(var + EPS)
    return out * (1.0 - LAMBDA_INIT)

@@ -1,0 +1,337 @@
+import math
+from contextlib import ExitStack
+
+import concourse.mybir as mybir
+from concourse.masks import make_identity
+
+F32 = mybir.dt.float32
+BF16 = mybir.dt.bfloat16
+U32 = mybir.dt.uint32
+U8 = mybir.dt.uint8
+FP8X4 = mybir.dt.float8_e4m3fn_x4
+ALU = mybir.AluOpType
+ACT = mybir.ActivationFunctionType
+AX = mybir.AxisListType
+
+P = 128
+H = 2
+S = 2048
+D = 256
+D2 = 128
+NT = S // P
+NB = S // 512
+SCALE = 1.0 / math.sqrt(D2)
+EPS = 1e-5
+GAIN = 0.2
+FLOPS = H * (2 * 2 * S * S * D2 + 2 * S * S * D)
+TOTAL = H * NT
+FIRST = (
+    (("k", 0, 0), ("q", 0, 0), ("k", 4, 0)),
+    (("k", 8, 0),),
+    (("k", 12, 0),),
+    (("k", 0, 1), ("q", 0, 1)),
+    (("k", 4, 1),),
+    (("k", 8, 1),),
+    (("k", 12, 1),),
+    (),
+)
+
+
+def tile_differentialattention_kernel(tc, query, key, value, lambda_params, out):
+    nc = tc.nc
+    with ExitStack() as ctx:
+        const = ctx.enter_context(tc.tile_pool(name="const", bufs=1))
+        raw = ctx.enter_context(tc.tile_pool(name="raw", bufs=2))
+        keep = ctx.enter_context(tc.tile_pool(name="keep", bufs=1))
+        work = ctx.enter_context(tc.tile_pool(name="work", bufs=4))
+        grp = ctx.enter_context(tc.tile_pool(name="grp", bufs=3))
+        small = ctx.enter_context(tc.tile_pool(name="small", bufs=6))
+        outp = ctx.enter_context(tc.tile_pool(name="outp", bufs=3))
+        psc = ctx.enter_context(tc.psum_pool(name="psc", bufs=3))
+        pat = ctx.enter_context(tc.psum_pool(name="pat", bufs=3))
+        pso = ctx.enter_context(tc.psum_pool(name="pso", bufs=2))
+        ctx.enter_context(tc.manual_schedule())
+
+        lam_bf = const.tile([P, H], BF16, name="lam_bf")
+        nc.sync.dma_start(out=lam_bf[:], in_=lambda_params.partition_broadcast(P))
+        kraw = {}
+        qraw = {}
+        vraw = {}
+        views = {}
+        for h in range(H):
+            kr = raw.tile([P, NT, D], BF16, tag="kraw")
+            qr = raw.tile([P, NT, D], BF16, tag="qraw")
+            vr = raw.tile([P, NT, D], BF16, tag="vraw")
+            kraw[h] = kr
+            qraw[h] = qr
+            vraw[h] = vr
+            views[("k", h)] = key[0, h].rearrange("(g p t) d -> p g t d", p=P, t=4)
+            views[("q", h)] = query[0, h].rearrange("(n p) d -> p n d", p=P)
+            views[("v", h)] = value[0, h].rearrange("(g p t) d -> p g t d", p=P, t=4)
+        nc.sync.dma_start(out=kraw[0][:, 0:4, :], in_=views[("k", 0)][:, 0])
+        nc.sync.dma_start(out=qraw[0][:, 0:4, :], in_=views[("q", 0)][:, 0:4, :])
+        for c in range(1, 4):
+            nc.sync.dma_start(out=kraw[0][:, 4 * c : 4 * c + 4, :], in_=views[("k", 0)][:, c])
+        nc.sync.dma_start(out=vraw[0][:].rearrange("p (g t) d -> p g t d", t=4), in_=views[("v", 0)])
+        nc.sync.dma_start(out=qraw[0][:, 4:16, :], in_=views[("q", 0)][:, 4:16, :])
+        nc.sync.dma_start(out=kraw[1][:].rearrange("p (g t) d -> p g t d", t=4), in_=views[("k", 1)])
+        nc.sync.dma_start(out=qraw[1][:], in_=views[("q", 1)])
+        nc.sync.dma_start(out=vraw[1][:].rearrange("p (g t) d -> p g t d", t=4), in_=views[("v", 1)])
+
+        ident_bf = const.tile([P, P], BF16, name="ident_bf")
+        make_identity(nc, ident_bf[:])
+        ident_f = const.tile([P, P], F32, name="ident_f")
+        make_identity(nc, ident_f[:])
+        mhalf = const.tile([P, 1], F32, name="mhalf")
+        nc.vector.memset(mhalf[:], -0.5)
+        warm = const.tile([P, 1], F32, name="warm")
+        nc.scalar.activation(out=warm[:], in_=mhalf[:], func=ACT.Exp)
+        neglam = const.tile([P, H], F32, name="neglam")
+        nc.vector.tensor_scalar(out=neglam[:], in0=lam_bf[:], scalar1=-1.0, scalar2=None, op0=ALU.mult)
+
+        qT = {}
+        kT = {}
+        vcod = {}
+        vpl = {}
+        vgrp = {}
+        for h in range(H):
+            for m in range(2):
+                a = keep.tile([P, S], BF16, name="qT%d%d" % (h, m))
+                b = keep.tile([P, S], BF16, name="kT%d%d" % (h, m))
+                qT[(h, m)] = a
+                kT[(h, m)] = b
+            c = keep.tile([P, NB, D], U32, name="vcod%d" % h, align_bytes=64)
+            d = keep.tile([P, NB, D], U8, name="vpl%d" % h, align_bytes=64)
+            e = keep.tile([P, NB, D, 4], BF16, name="vgrp%d" % h, align_bytes=64)
+            vcod[h] = c
+            vpl[h] = d
+            vgrp[h] = e
+
+        def prep_unit(kind, h, n0, m):
+            src = kraw[h] if kind == "k" else qraw[h]
+            dst = kT[(h, m)] if kind == "k" else qT[(h, m)]
+            pt = pat.tile([P, 4, P], BF16, tag="at")
+            for a in range(4):
+                nc.tensor.transpose(pt[:, a, :], src[:, n0 + a, m * P : (m + 1) * P], ident_bf[:])
+            nc.scalar.copy(out=dst[:, n0 * P : (n0 + 4) * P], in_=pt[:].rearrange("p a q -> p (a q)"))
+
+        def regroup_v(h, g):
+            nc.gpsimd.tensor_scalar(
+                out=vgrp[h][:, g],
+                in0=vraw[h][:, 4 * g : 4 * g + 4, :].rearrange("p t d -> p d t"),
+                scalar1=1.0,
+                scalar2=0.0,
+                op0=ALU.mult,
+                op1=ALU.add,
+            )
+
+        def quant_v(h):
+            nc.vector.quantize_mx(
+                out=vcod[h][:].rearrange("p g d -> p (g d)").bitcast(FP8X4),
+                scales=vpl[h][:].rearrange("p g d -> p (g d)"),
+                in_=vgrp[h][:].rearrange("p g d t -> p (g d t)"),
+            )
+
+        st = {}
+
+        def live(x):
+            return 0 <= x < TOTAL
+
+        def score(x, s):
+            h, i = divmod(x, NT)
+            m, j = divmod(s, NB)
+            if s == 0:
+                st[x] = {}
+            rec = st[x]
+            if j == 0:
+                sc = work.tile([P, S], F32, tag="sc%d" % m)
+                mn = small.tile([P, NB], F32, tag="mn%d" % m)
+                rec["sc%d" % m] = sc
+                rec["mn%d" % m] = mn
+            sc = rec["sc%d" % m]
+            mn = rec["mn%d" % m]
+            ps = psc.tile([P, 512], F32, tag="ps")
+            nc.tensor.matmul(
+                ps[:],
+                lhsT=qT[(h, m)][:, i * P : (i + 1) * P],
+                rhs=kT[(h, m)][:, j * 512 : (j + 1) * 512],
+                start=True,
+                stop=True,
+            )
+            nc.vector.tensor_scalar(
+                out=sc[:, j * 512 : (j + 1) * 512],
+                in0=ps[:],
+                scalar1=-SCALE,
+                scalar2=None,
+                op0=ALU.mult,
+                op1=ALU.min,
+                accum_out=mn[:, j : j + 1],
+            )
+            if j == NB - 1:
+                nm = small.tile([P, 1], F32, tag="nm%d" % m)
+                nc.vector.tensor_reduce(out=nm[:], in_=mn[:], axis=AX.X, op=ALU.min)
+                rec["nm%d" % m] = nm
+
+        def expo(x, m):
+            rec = st[x]
+            sc = rec["sc%d" % m]
+            sm = small.tile([P, 1], F32, tag="sm%d" % m)
+            nc.scalar.activation(out=sc[:], in_=sc[:], func=ACT.Exp, bias=rec["nm%d" % m][:], scale=-1.0, accum_out=sm[:])
+            rec["sm%d" % m] = sm
+
+        def recip(x, m):
+            rec = st[x]
+            rr = small.tile([P, 1], F32, tag="rr%d" % m)
+            nc.vector.reciprocal(out=rr[:], in_=rec["sm%d" % m][:])
+            rec["rr%d" % m] = rr
+
+        def norm_map(x, m):
+            h, i = divmod(x, NT)
+            rec = st[x]
+            sc = rec["sc%d" % m]
+            eng = nc.vector if x == TOTAL - 1 else nc.gpsimd
+            if m == 0:
+                eng.tensor_scalar(out=sc[:], in0=sc[:], scalar1=rec["rr0"][:], scalar2=0.0, op0=ALU.mult, op1=ALU.add)
+            else:
+                eng.tensor_scalar(
+                    out=sc[:], in0=sc[:], scalar1=rec["rr1"][:], scalar2=neglam[:, h : h + 1], op0=ALU.mult, op1=ALU.mult
+                )
+
+        def turn(x, s):
+            rec = st[x]
+            g, half = divmod(s, 2)
+            if s == 0:
+                gr = grp.tile([P, NB, P, 4], BF16, tag="gr", align_bytes=64)
+                rec["gr"] = gr
+            if half == 0:
+                at = pat.tile([P, 4, P], F32, tag="at")
+                rec["at%d" % g] = at
+            at = rec["at%d" % g]
+            for t in (2 * half, 2 * half + 1):
+                c0 = (4 * g + t) * P
+                nc.tensor.matmul(
+                    at[:, t, :], lhsT=rec["sc0"][:, c0 : c0 + P], rhs=ident_f[:], is_transpose=True, start=True, stop=False
+                )
+                nc.tensor.matmul(
+                    at[:, t, :], lhsT=rec["sc1"][:, c0 : c0 + P], rhs=ident_f[:], is_transpose=True, start=False, stop=True
+                )
+
+        def copy_group(x, g, eng):
+            rec = st[x]
+            src = rec["at%d" % g][:].rearrange("p t q -> p q t")
+            if eng == "s":
+                nc.scalar.copy(out=rec["gr"][:, g], in_=src)
+            else:
+                nc.vector.tensor_copy(out=rec["gr"][:, g], in_=src)
+
+        def quant(x):
+            rec = st[x]
+            cod = grp.tile([P, NB * P], U32, tag="cod", align_bytes=64)
+            pl = grp.tile([P, NB * P], U8, tag="pl", align_bytes=64)
+            nc.vector.quantize_mx(
+                out=cod[:].bitcast(FP8X4), scales=pl[:], in_=rec["gr"][:].rearrange("p g q t -> p (g q t)")
+            )
+            rec["cod"] = cod
+            rec["pl"] = pl
+
+        def pv(x):
+            h, i = divmod(x, NT)
+            rec = st[x]
+            o = pso.tile([P, D], F32, tag="o")
+            for g in range(NB):
+                nc.tensor.matmul_mx(
+                    out=o[:],
+                    lhsT=rec["cod"][:, g * P : (g + 1) * P].bitcast(FP8X4),
+                    lhsT_scale=rec["pl"][:, g * P : (g + 1) * P],
+                    rhs=vcod[h][:, g, :].bitcast(FP8X4),
+                    rhs_scale=vpl[h][:, g, :],
+                    start=(g == 0),
+                    stop=(g == NB - 1),
+                )
+            rec["o"] = o
+
+        def stats(x):
+            rec = st[x]
+            bs = small.tile([P, 6], F32, tag="bs")
+            nc.vector.bn_stats(out=bs[:], in_=rec["o"][:])
+            mv = small.tile([P, 2], F32, tag="mv")
+            nc.vector.bn_aggr(out=mv[:], in_=bs[:])
+            v25 = small.tile([P, 1], F32, tag="v25")
+            nc.gpsimd.tensor_scalar(
+                out=v25[:], in0=mv[:, 1:2], scalar1=1.0 / (GAIN * GAIN), scalar2=EPS / (GAIN * GAIN), op0=ALU.mult, op1=ALU.add
+            )
+            rs = small.tile([P, 1], F32, tag="rs")
+            nc.gpsimd.tensor_tensor(out=rs[:], in0=v25[:], in1=mhalf[:], op=ALU.pow)
+            nb = small.tile([P, 1], F32, tag="nb")
+            nc.gpsimd.tensor_scalar(out=nb[:], in0=mv[:, 0:1], scalar1=rs[:], scalar2=-1.0, op0=ALU.mult, op1=ALU.mult)
+            rec["rs"] = rs
+            rec["nb"] = nb
+
+        def finish(x):
+            h, i = divmod(x, NT)
+            rec = st[x]
+            res = outp.tile([P, D], F32, tag="res")
+            nc.scalar.activation(out=res[:], in_=rec["o"][:], func=ACT.Identity, bias=rec["nb"][:], scale=rec["rs"][:])
+            nc.sync.dma_start(out=out[0, h, i * P : (i + 1) * P, :], in_=res[:])
+
+        later = []
+        for n0 in (4, 8, 12):
+            for m in range(2):
+                later.append(("q", 0, n0, m))
+        for n0 in (0, 4, 8, 12):
+            for m in range(2):
+                later.append(("k", 1, n0, m))
+        for n0 in (0, 4, 8, 12):
+            for m in range(2):
+                later.append(("q", 1, n0, m))
+        pos = [0]
+
+        def next_unit():
+            if pos[0] < len(later):
+                u = later[pos[0]]
+                pos[0] += 1
+                prep_unit(u[0], u[1], u[2], u[3])
+
+        for g in range(NB):
+            regroup_v(0, g)
+
+        for x in range(TOTAL + 5):
+            if live(x - 1):
+                norm_map(x - 1, 0)
+                expo(x - 1, 1)
+            for s in range(8):
+                if x == 0:
+                    for u in FIRST[s]:
+                        prep_unit(u[0], 0, u[1], u[2])
+                if live(x):
+                    score(x, s)
+                if live(x - 2):
+                    turn(x - 2, s)
+                    if s in (1, 3, 5):
+                        copy_group(x - 2, s // 2, "s")
+                if s == 1 and live(x - 4):
+                    finish(x - 4)
+                if s == (3 if x > 0 else 7) and live(x):
+                    expo(x, 0)
+                if s == 2 and live(x - 3):
+                    pv(x - 3)
+                if s == 4 and live(x - 3):
+                    stats(x - 3)
+                if s == 3 and live(x - 1):
+                    recip(x - 1, 1)
+                    norm_map(x - 1, 1)
+            if 1 <= x:
+                next_unit()
+                if x <= 3:
+                    next_unit()
+            if 3 <= x <= 6:
+                regroup_v(1, x - 3)
+            if live(x - 2):
+                copy_group(x - 2, 3, "s")
+                quant(x - 2)
+            if x == 1:
+                quant_v(0)
+            if x == 8:
+                quant_v(1)
+            if live(x):
+                recip(x, 0)

@@ -20,6 +20,7 @@ D = 256
 D2 = 128
 NT = S // P
 NB = S // 512
+HALF = S // 2
 SCALE = 1.0 / math.sqrt(D2)
 EPS = 1e-5
 GAIN = 0.2
@@ -43,7 +44,7 @@ def tile_differentialattention_kernel(tc, query, key, value, lambda_params, out)
         const = ctx.enter_context(tc.tile_pool(name="const", bufs=1))
         raw = ctx.enter_context(tc.tile_pool(name="raw", bufs=2))
         keep = ctx.enter_context(tc.tile_pool(name="keep", bufs=1))
-        work = ctx.enter_context(tc.tile_pool(name="work", bufs=4))
+        work = ctx.enter_context(tc.tile_pool(name="work", bufs=5))
         grp = ctx.enter_context(tc.tile_pool(name="grp", bufs=3))
         small = ctx.enter_context(tc.tile_pool(name="small", bufs=6))
         outp = ctx.enter_context(tc.tile_pool(name="outp", bufs=3))
@@ -53,41 +54,40 @@ def tile_differentialattention_kernel(tc, query, key, value, lambda_params, out)
         ctx.enter_context(tc.manual_schedule())
 
         lam_bf = const.tile([P, H], BF16, name="lam_bf")
-        nc.sync.dma_start(out=lam_bf[:], in_=lambda_params.partition_broadcast(P))
         kraw = {}
         qraw = {}
         vraw = {}
         views = {}
         for h in range(H):
-            kr = raw.tile([P, NT, D], BF16, tag="kraw")
+            kr = raw.tile([P, NB, 4, D], BF16, tag="kraw")
             qr = raw.tile([P, NT, D], BF16, tag="qraw")
-            vr = raw.tile([P, NT, D], BF16, tag="vraw")
+            vr = raw.tile([P, NB, 4, D], BF16, tag="vraw")
             kraw[h] = kr
             qraw[h] = qr
             vraw[h] = vr
             views[("k", h)] = key[0, h].rearrange("(g p t) d -> p g t d", p=P, t=4)
             views[("q", h)] = query[0, h].rearrange("(n p) d -> p n d", p=P)
             views[("v", h)] = value[0, h].rearrange("(g p t) d -> p g t d", p=P, t=4)
-        nc.sync.dma_start(out=kraw[0][:, 0:4, :], in_=views[("k", 0)][:, 0])
+        nc.sync.dma_start(out=kraw[0][:, 0], in_=views[("k", 0)][:, 0])
         nc.sync.dma_start(out=qraw[0][:, 0:4, :], in_=views[("q", 0)][:, 0:4, :])
         for c in range(1, 4):
-            nc.sync.dma_start(out=kraw[0][:, 4 * c : 4 * c + 4, :], in_=views[("k", 0)][:, c])
-        nc.sync.dma_start(out=vraw[0][:].rearrange("p (g t) d -> p g t d", t=4), in_=views[("v", 0)])
+            nc.sync.dma_start(out=kraw[0][:, c], in_=views[("k", 0)][:, c])
+        nc.sync.dma_start(out=lam_bf[:], in_=lambda_params.partition_broadcast(P))
+        nc.sync.dma_start(out=vraw[0][:], in_=views[("v", 0)])
         nc.sync.dma_start(out=qraw[0][:, 4:16, :], in_=views[("q", 0)][:, 4:16, :])
-        nc.sync.dma_start(out=kraw[1][:].rearrange("p (g t) d -> p g t d", t=4), in_=views[("k", 1)])
+        nc.sync.dma_start(out=kraw[1][:], in_=views[("k", 1)])
         nc.sync.dma_start(out=qraw[1][:], in_=views[("q", 1)])
-        nc.sync.dma_start(out=vraw[1][:].rearrange("p (g t) d -> p g t d", t=4), in_=views[("v", 1)])
+        nc.sync.dma_start(out=vraw[1][:], in_=views[("v", 1)])
 
         ident_bf = const.tile([P, P], BF16, name="ident_bf")
         make_identity(nc, ident_bf[:])
         ident_f = const.tile([P, P], F32, name="ident_f")
         make_identity(nc, ident_f[:])
-        mhalf = const.tile([P, 1], F32, name="mhalf")
+        mhalf = const.tile([P, 2], F32, name="mhalf")
         nc.vector.memset(mhalf[:], -0.5)
         warm = const.tile([P, 1], F32, name="warm")
-        nc.scalar.activation(out=warm[:], in_=mhalf[:], func=ACT.Exp)
+        nc.scalar.activation(out=warm[:], in_=mhalf[:, 0:1], func=ACT.Exp)
         neglam = const.tile([P, H], F32, name="neglam")
-        nc.vector.tensor_scalar(out=neglam[:], in0=lam_bf[:], scalar1=-1.0, scalar2=None, op0=ALU.mult)
 
         qT = {}
         kT = {}
@@ -107,18 +107,24 @@ def tile_differentialattention_kernel(tc, query, key, value, lambda_params, out)
             vpl[h] = d
             vgrp[h] = e
 
-        def prep_unit(kind, h, n0, m):
-            src = kraw[h] if kind == "k" else qraw[h]
+        def copy(eng, dst, src):
+            if eng == "s":
+                nc.scalar.copy(out=dst, in_=src)
+            else:
+                nc.vector.tensor_copy(out=dst, in_=src)
+
+        def prep_unit(kind, h, n0, m, eng):
             dst = kT[(h, m)] if kind == "k" else qT[(h, m)]
             pt = pat.tile([P, 4, P], BF16, tag="at")
             for a in range(4):
-                nc.tensor.transpose(pt[:, a, :], src[:, n0 + a, m * P : (m + 1) * P], ident_bf[:])
-            nc.scalar.copy(out=dst[:, n0 * P : (n0 + 4) * P], in_=pt[:].rearrange("p a q -> p (a q)"))
+                src = kraw[h][:, n0 // 4, a] if kind == "k" else qraw[h][:, n0 + a]
+                nc.tensor.transpose(pt[:, a, :], src[:, m * P : (m + 1) * P], ident_bf[:])
+            copy(eng, dst[:, n0 * P : (n0 + 4) * P], pt[:].rearrange("p a q -> p (a q)"))
 
         def regroup_v(h, g):
             nc.gpsimd.tensor_scalar(
                 out=vgrp[h][:, g],
-                in0=vraw[h][:, 4 * g : 4 * g + 4, :].rearrange("p t d -> p d t"),
+                in0=vraw[h][:, g].rearrange("p t d -> p d t"),
                 scalar1=1.0,
                 scalar2=0.0,
                 op0=ALU.mult,
@@ -141,15 +147,14 @@ def tile_differentialattention_kernel(tc, query, key, value, lambda_params, out)
             h, i = divmod(x, NT)
             m, j = divmod(s, NB)
             if s == 0:
-                st[x] = {}
+                sm = small.tile([P, 2], F32, tag="sm")
+                st[x] = {"sm": sm}
             rec = st[x]
             if j == 0:
                 sc = work.tile([P, S], F32, tag="sc%d" % m)
                 mn = small.tile([P, NB], F32, tag="mn%d" % m)
                 rec["sc%d" % m] = sc
                 rec["mn%d" % m] = mn
-            sc = rec["sc%d" % m]
-            mn = rec["mn%d" % m]
             ps = psc.tile([P, 512], F32, tag="ps")
             nc.tensor.matmul(
                 ps[:],
@@ -159,70 +164,66 @@ def tile_differentialattention_kernel(tc, query, key, value, lambda_params, out)
                 stop=True,
             )
             nc.vector.tensor_scalar(
-                out=sc[:, j * 512 : (j + 1) * 512],
+                out=rec["sc%d" % m][:, j * 512 : (j + 1) * 512],
                 in0=ps[:],
                 scalar1=-SCALE,
                 scalar2=None,
                 op0=ALU.mult,
                 op1=ALU.min,
-                accum_out=mn[:, j : j + 1],
+                accum_out=rec["mn%d" % m][:, j : j + 1],
             )
-            if j == NB - 1:
-                nm = small.tile([P, 1], F32, tag="nm%d" % m)
-                nc.vector.tensor_reduce(out=nm[:], in_=mn[:], axis=AX.X, op=ALU.min)
-                rec["nm%d" % m] = nm
+
+        def rowmin(x, m):
+            rec = st[x]
+            nm = small.tile([P, 1], F32, tag="nm%d" % m)
+            nc.vector.tensor_reduce(out=nm[:], in_=rec["mn%d" % m][:], axis=AX.X, op=ALU.min)
+            rec["nm%d" % m] = nm
 
         def expo(x, m):
             rec = st[x]
             sc = rec["sc%d" % m]
-            sm = small.tile([P, 1], F32, tag="sm%d" % m)
-            nc.scalar.activation(out=sc[:], in_=sc[:], func=ACT.Exp, bias=rec["nm%d" % m][:], scale=-1.0, accum_out=sm[:])
-            rec["sm%d" % m] = sm
+            nc.scalar.activation(
+                out=sc[:], in_=sc[:], func=ACT.Exp, bias=rec["nm%d" % m][:], scale=-1.0, accum_out=rec["sm"][:, m : m + 1]
+            )
 
-        def recip(x, m):
+        def recip(x):
             rec = st[x]
-            rr = small.tile([P, 1], F32, tag="rr%d" % m)
-            nc.vector.reciprocal(out=rr[:], in_=rec["sm%d" % m][:])
-            rec["rr%d" % m] = rr
+            rr = small.tile([P, 2], F32, tag="rr")
+            nc.vector.reciprocal(out=rr[:], in_=rec["sm"][:])
+            rec["rr"] = rr
 
-        def norm_map(x, m):
-            h, i = divmod(x, NT)
+        def norm_maps(x, eng):
+            h = x // NT
             rec = st[x]
-            sc = rec["sc%d" % m]
-            eng = nc.vector if x == TOTAL - 1 else nc.gpsimd
-            if m == 0:
-                eng.tensor_scalar(out=sc[:], in0=sc[:], scalar1=rec["rr0"][:], scalar2=0.0, op0=ALU.mult, op1=ALU.add)
-            else:
+            rr = rec["rr"]
+            for c in range(2):
+                cols = slice(c * HALF, (c + 1) * HALF)
+                a = rec["sc0"][:, cols]
+                b = rec["sc1"][:, cols]
+                eng.tensor_scalar(out=a, in0=a, scalar1=rr[:, 0:1], scalar2=0.0, op0=ALU.mult, op1=ALU.add)
                 eng.tensor_scalar(
-                    out=sc[:], in0=sc[:], scalar1=rec["rr1"][:], scalar2=neglam[:, h : h + 1], op0=ALU.mult, op1=ALU.mult
+                    out=b, in0=b, scalar1=rr[:, 1:2], scalar2=neglam[:, h : h + 1], op0=ALU.mult, op1=ALU.mult
                 )
 
-        def turn(x, s):
+        def turn(x, g):
             rec = st[x]
-            g, half = divmod(s, 2)
-            if s == 0:
+            if g == 0:
                 gr = grp.tile([P, NB, P, 4], BF16, tag="gr", align_bytes=64)
                 rec["gr"] = gr
-            if half == 0:
-                at = pat.tile([P, 4, P], F32, tag="at")
-                rec["at%d" % g] = at
-            at = rec["at%d" % g]
-            for t in (2 * half, 2 * half + 1):
-                c0 = (4 * g + t) * P
+            at = pat.tile([P, 4, P], F32, tag="at")
+            rec["at%d" % g] = at
+            for t in range(4):
+                cols = slice((4 * g + t) * P, (4 * g + t + 1) * P)
                 nc.tensor.matmul(
-                    at[:, t, :], lhsT=rec["sc0"][:, c0 : c0 + P], rhs=ident_f[:], is_transpose=True, start=True, stop=False
+                    at[:, t, :], lhsT=rec["sc0"][:, cols], rhs=ident_f[:], is_transpose=True, start=True, stop=False
                 )
                 nc.tensor.matmul(
-                    at[:, t, :], lhsT=rec["sc1"][:, c0 : c0 + P], rhs=ident_f[:], is_transpose=True, start=False, stop=True
+                    at[:, t, :], lhsT=rec["sc1"][:, cols], rhs=ident_f[:], is_transpose=True, start=False, stop=True
                 )
 
         def copy_group(x, g, eng):
             rec = st[x]
-            src = rec["at%d" % g][:].rearrange("p t q -> p q t")
-            if eng == "s":
-                nc.scalar.copy(out=rec["gr"][:, g], in_=src)
-            else:
-                nc.vector.tensor_copy(out=rec["gr"][:, g], in_=src)
+            copy(eng, rec["gr"][:, g], rec["at%d" % g][:].rearrange("p t q -> p q t"))
 
         def quant(x):
             rec = st[x]
@@ -235,12 +236,16 @@ def tile_differentialattention_kernel(tc, query, key, value, lambda_params, out)
             rec["pl"] = pl
 
         def pv(x):
-            h, i = divmod(x, NT)
+            h = x // NT
             rec = st[x]
-            o = pso.tile([P, D], F32, tag="o")
+            if x % 2 == 0 or x == TOTAL - 1:
+                o2 = pso.tile([P, 2, D], F32, tag="o2")
+                rec["o2"] = o2
+            else:
+                rec["o2"] = st[x - 1]["o2"]
             for g in range(NB):
                 nc.tensor.matmul_mx(
-                    out=o[:],
+                    out=rec["o2"][:, x % 2, :],
                     lhsT=rec["cod"][:, g * P : (g + 1) * P].bitcast(FP8X4),
                     lhsT_scale=rec["pl"][:, g * P : (g + 1) * P],
                     rhs=vcod[h][:, g, :].bitcast(FP8X4),
@@ -248,90 +253,110 @@ def tile_differentialattention_kernel(tc, query, key, value, lambda_params, out)
                     start=(g == 0),
                     stop=(g == NB - 1),
                 )
-            rec["o"] = o
 
-        def stats(x):
-            rec = st[x]
-            bs = small.tile([P, 6], F32, tag="bs")
-            nc.vector.bn_stats(out=bs[:], in_=rec["o"][:])
-            mv = small.tile([P, 2], F32, tag="mv")
-            nc.vector.bn_aggr(out=mv[:], in_=bs[:])
-            v25 = small.tile([P, 1], F32, tag="v25")
+        def stats(x0, n):
+            rec = st[x0]
+            bs = small.tile([P, 2, 6], F32, tag="bs")
+            mv = small.tile([P, 2, 2], F32, tag="mv")
+            for k in range(n):
+                nc.vector.bn_stats(out=bs[:, k, :], in_=st[x0 + k]["o2"][:, (x0 + k) % 2, :])
+            for k in range(n):
+                nc.vector.bn_aggr(out=mv[:, k, :], in_=bs[:, k, :])
+            v25 = small.tile([P, 2], F32, tag="v25")
             nc.gpsimd.tensor_scalar(
-                out=v25[:], in0=mv[:, 1:2], scalar1=1.0 / (GAIN * GAIN), scalar2=EPS / (GAIN * GAIN), op0=ALU.mult, op1=ALU.add
+                out=v25[:, 0:n],
+                in0=mv[:, 0:n, 1],
+                scalar1=1.0 / (GAIN * GAIN),
+                scalar2=EPS / (GAIN * GAIN),
+                op0=ALU.mult,
+                op1=ALU.add,
             )
-            rs = small.tile([P, 1], F32, tag="rs")
-            nc.gpsimd.tensor_tensor(out=rs[:], in0=v25[:], in1=mhalf[:], op=ALU.pow)
-            nb = small.tile([P, 1], F32, tag="nb")
-            nc.gpsimd.tensor_scalar(out=nb[:], in0=mv[:, 0:1], scalar1=rs[:], scalar2=-1.0, op0=ALU.mult, op1=ALU.mult)
+            rs = small.tile([P, 2], F32, tag="rs")
+            nc.gpsimd.tensor_tensor(out=rs[:, 0:n], in0=v25[:, 0:n], in1=mhalf[:, 0:n], op=ALU.pow)
+            rec["mv"] = mv
             rec["rs"] = rs
-            rec["nb"] = nb
 
-        def finish(x):
-            h, i = divmod(x, NT)
-            rec = st[x]
-            res = outp.tile([P, D], F32, tag="res")
-            nc.scalar.activation(out=res[:], in_=rec["o"][:], func=ACT.Identity, bias=rec["nb"][:], scale=rec["rs"][:])
-            nc.sync.dma_start(out=out[0, h, i * P : (i + 1) * P, :], in_=res[:])
+        def finish(x0, n):
+            h, i = divmod(x0, NT)
+            rec = st[x0]
+            res = outp.tile([P, 2, D], F32, tag="res")
+            for k in range(n):
+                nc.vector.tensor_scalar(
+                    out=res[:, k, :],
+                    in0=st[x0 + k]["o2"][:, (x0 + k) % 2, :],
+                    scalar1=rec["mv"][:, k, 0:1],
+                    scalar2=rec["rs"][:, k : k + 1],
+                    op0=ALU.subtract,
+                    op1=ALU.mult,
+                )
+            nc.sync.dma_start(
+                out=out[0, h, i * P : (i + n) * P, :].rearrange("(n p) d -> p n d", p=P), in_=res[:, 0:n, :]
+            )
 
         later = []
         for n0 in (4, 8, 12):
             for m in range(2):
                 later.append(("q", 0, n0, m))
-        for n0 in (0, 4, 8, 12):
-            for m in range(2):
-                later.append(("k", 1, n0, m))
-        for n0 in (0, 4, 8, 12):
-            for m in range(2):
-                later.append(("q", 1, n0, m))
+        for kind in ("k", "q"):
+            for n0 in (0, 4, 8, 12):
+                for m in range(2):
+                    later.append((kind, 1, n0, m))
         pos = [0]
 
         def next_unit():
             if pos[0] < len(later):
                 u = later[pos[0]]
                 pos[0] += 1
-                prep_unit(u[0], u[1], u[2], u[3])
+                prep_unit(u[0], u[1], u[2], u[3], "v")
 
+        nc.gpsimd.tensor_scalar(out=neglam[:], in0=lam_bf[:], scalar1=-1.0, scalar2=0.0, op0=ALU.mult, op1=ALU.add)
         for g in range(NB):
             regroup_v(0, g)
 
-        for x in range(TOTAL + 5):
-            if live(x - 1):
-                norm_map(x - 1, 0)
-                expo(x - 1, 1)
+        turns = [0]
+        for x in range(TOTAL + 4):
+            last_tiles = x - 3 >= TOTAL - 2
             for s in range(8):
                 if x == 0:
                     for u in FIRST[s]:
-                        prep_unit(u[0], 0, u[1], u[2])
+                        prep_unit(u[0], 0, u[1], u[2], "sv"[turns[0] % 2])
+                        turns[0] += 1
+                if s == 7 and live(x - 4):
+                    pv(x - 4)
                 if live(x):
                     score(x, s)
-                if live(x - 2):
-                    turn(x - 2, s)
-                    if s in (1, 3, 5):
-                        copy_group(x - 2, s // 2, "s")
-                if s == 1 and live(x - 4):
-                    finish(x - 4)
-                if s == (3 if x > 0 else 7) and live(x):
-                    expo(x, 0)
-                if s == 2 and live(x - 3):
-                    pv(x - 3)
-                if s == 4 and live(x - 3):
-                    stats(x - 3)
+                if s == 0 and live(x - 1):
+                    rowmin(x - 1, 1)
+                    expo(x - 1, 0)
+                if s == 2:
+                    if live(x - 4):
+                        quant(x - 4)
+                    if live(x - 2):
+                        recip(x - 2)
+                        norm_maps(x - 2, nc.vector if x - 2 >= TOTAL - 2 else nc.gpsimd)
+                    if 3 <= x <= 6:
+                        regroup_v(1, x - 3)
+                if s == 4 and 0 <= x - 6 < TOTAL - 2 and x % 2 == 0:
+                    stats(x - 6, 2)
+                if s == 5 and live(x):
+                    rowmin(x, 0)
+                if s == 5 and 0 <= x - 7 < TOTAL - 2 and x % 2 == 1:
+                    finish(x - 7, 2)
+                if s % 2 == 1 and live(x - 3):
+                    g = s // 2
+                    turn(x - 3, g)
+                    copy_group(x - 3, g, "v" if last_tiles and g % 2 else "s")
                 if s == 3 and live(x - 1):
-                    recip(x - 1, 1)
-                    norm_map(x - 1, 1)
-            if 1 <= x:
+                    expo(x - 1, 1)
+            if x >= 1:
                 next_unit()
                 if x <= 3:
                     next_unit()
-            if 3 <= x <= 6:
-                regroup_v(1, x - 3)
-            if live(x - 2):
-                copy_group(x - 2, 3, "s")
-                quant(x - 2)
-            if x == 1:
+            if x == 2:
                 quant_v(0)
             if x == 8:
                 quant_v(1)
-            if live(x):
-                recip(x, 0)
+        for x in (TOTAL - 2, TOTAL - 1):
+            stats(x, 1)
+        for x in (TOTAL - 2, TOTAL - 1):
+            finish(x, 1)

@@ -192,18 +192,15 @@ def tile_differentialattention_kernel(tc, query, key, value, lambda_params, out)
             nc.vector.reciprocal(out=rr[:], in_=rec["sm"][:])
             rec["rr"] = rr
 
-        def norm_maps(x, eng):
+        def norm_half(x, c, eng):
             h = x // NT
             rec = st[x]
             rr = rec["rr"]
-            for c in range(2):
-                cols = slice(c * HALF, (c + 1) * HALF)
-                a = rec["sc0"][:, cols]
-                b = rec["sc1"][:, cols]
-                eng.tensor_scalar(out=a, in0=a, scalar1=rr[:, 0:1], scalar2=0.0, op0=ALU.mult, op1=ALU.add)
-                eng.tensor_scalar(
-                    out=b, in0=b, scalar1=rr[:, 1:2], scalar2=neglam[:, h : h + 1], op0=ALU.mult, op1=ALU.mult
-                )
+            cols = slice(c * HALF, (c + 1) * HALF)
+            a = rec["sc0"][:, cols]
+            b = rec["sc1"][:, cols]
+            eng.tensor_scalar(out=a, in0=a, scalar1=rr[:, 0:1], scalar2=0.0, op0=ALU.mult, op1=ALU.add)
+            eng.tensor_scalar(out=b, in0=b, scalar1=rr[:, 1:2], scalar2=neglam[:, h : h + 1], op0=ALU.mult, op1=ALU.mult)
 
         def turn(x, g):
             rec = st[x]
@@ -225,15 +222,19 @@ def tile_differentialattention_kernel(tc, query, key, value, lambda_params, out)
             rec = st[x]
             copy(eng, rec["gr"][:, g], rec["at%d" % g][:].rearrange("p t q -> p q t"))
 
-        def quant(x):
+        def quant(x, g0=0, n=NB):
             rec = st[x]
-            cod = grp.tile([P, NB * P], U32, tag="cod", align_bytes=64)
-            pl = grp.tile([P, NB * P], U8, tag="pl", align_bytes=64)
+            if g0 == 0:
+                cod = grp.tile([P, NB * P], U32, tag="cod", align_bytes=64)
+                pl = grp.tile([P, NB * P], U8, tag="pl", align_bytes=64)
+                rec["cod"] = cod
+                rec["pl"] = pl
+            cols = slice(g0 * P, (g0 + n) * P)
             nc.vector.quantize_mx(
-                out=cod[:].bitcast(FP8X4), scales=pl[:], in_=rec["gr"][:].rearrange("p g q t -> p (g q t)")
+                out=rec["cod"][:, cols].bitcast(FP8X4),
+                scales=rec["pl"][:, cols],
+                in_=rec["gr"][:, g0 : g0 + n].rearrange("p g q t -> p (g q t)"),
             )
-            rec["cod"] = cod
-            rec["pl"] = pl
 
         def pv(x):
             h = x // NT
@@ -314,8 +315,7 @@ def tile_differentialattention_kernel(tc, query, key, value, lambda_params, out)
             regroup_v(0, g)
 
         turns = [0]
-        for x in range(TOTAL + 4):
-            last_tiles = x - 3 >= TOTAL - 2
+        for x in range(TOTAL):
             for s in range(8):
                 if x == 0:
                     for u in FIRST[s]:
@@ -323,8 +323,7 @@ def tile_differentialattention_kernel(tc, query, key, value, lambda_params, out)
                         turns[0] += 1
                 if s == 7 and live(x - 4):
                     pv(x - 4)
-                if live(x):
-                    score(x, s)
+                score(x, s)
                 if s == 0 and live(x - 1):
                     rowmin(x - 1, 1)
                     expo(x - 1, 0)
@@ -333,19 +332,20 @@ def tile_differentialattention_kernel(tc, query, key, value, lambda_params, out)
                         quant(x - 4)
                     if live(x - 2):
                         recip(x - 2)
-                        norm_maps(x - 2, nc.vector if x - 2 >= TOTAL - 2 else nc.gpsimd)
+                        norm_half(x - 2, 0, nc.gpsimd)
+                        norm_half(x - 2, 1, nc.gpsimd)
                     if 3 <= x <= 6:
                         regroup_v(1, x - 3)
-                if s == 4 and 0 <= x - 6 < TOTAL - 2 and x % 2 == 0:
+                if s == 4 and live(x - 6) and x % 2 == 0:
                     stats(x - 6, 2)
-                if s == 5 and live(x):
+                if s == 5:
                     rowmin(x, 0)
-                if s == 5 and 0 <= x - 7 < TOTAL - 2 and x % 2 == 1:
+                if s == 5 and live(x - 7) and x % 2 == 1:
                     finish(x - 7, 2)
                 if s % 2 == 1 and live(x - 3):
                     g = s // 2
                     turn(x - 3, g)
-                    copy_group(x - 3, g, "v" if last_tiles and g % 2 else "s")
+                    copy_group(x - 3, g, "s")
                 if s == 3 and live(x - 1):
                     expo(x - 1, 1)
             if x >= 1:
@@ -356,7 +356,53 @@ def tile_differentialattention_kernel(tc, query, key, value, lambda_params, out)
                 quant_v(0)
             if x == 8:
                 quant_v(1)
-        for x in (TOTAL - 2, TOTAL - 1):
-            stats(x, 1)
-        for x in (TOTAL - 2, TOTAL - 1):
-            finish(x, 1)
+
+        z = TOTAL - 1
+        rowmin(z, 1)
+        expo(z, 0)
+        expo(z, 1)
+        stats(z - 5, 2)
+        turn(z - 2, 0)
+        copy_group(z - 2, 0, "v")
+        turn(z - 2, 1)
+        copy_group(z - 2, 1, "v")
+        quant(z - 3)
+        recip(z - 1)
+        norm_half(z - 1, 0, nc.vector)
+        norm_half(z - 1, 1, nc.gpsimd)
+        pv(z - 3)
+        for g in (2, 3):
+            turn(z - 2, g)
+            copy_group(z - 2, g, "v")
+        turn(z - 1, 0)
+        copy_group(z - 1, 0, "v")
+        turn(z - 1, 1)
+        copy_group(z - 1, 1, "v")
+        recip(z)
+        norm_half(z, 0, nc.vector)
+        quant(z - 2)
+        norm_half(z, 1, nc.vector)
+        for g in (2, 3):
+            turn(z - 1, g)
+            copy_group(z - 1, g, "s")
+        pv(z - 2)
+        finish(z - 5, 2)
+        turn(z, 0)
+        copy_group(z, 0, "v")
+        turn(z, 1)
+        copy_group(z, 1, "s")
+        quant(z - 1)
+        turn(z, 2)
+        copy_group(z, 2, "v")
+        turn(z, 3)
+        copy_group(z, 3, "s")
+        stats(z - 3, 2)
+        pv(z - 1)
+        quant(z, 0, 2)
+        quant(z, 2, 2)
+        stats(z - 1, 1)
+        finish(z - 3, 2)
+        pv(z)
+        stats(z, 1)
+        finish(z - 1, 1)
+        finish(z, 1)

@@ -202,14 +202,16 @@ def tile_differentialattention_kernel(tc, query, key, value, lambda_params, out)
             eng.tensor_scalar(out=a, in0=a, scalar1=rr[:, 0:1], scalar2=0.0, op0=ALU.mult, op1=ALU.add)
             eng.tensor_scalar(out=b, in0=b, scalar1=rr[:, 1:2], scalar2=neglam[:, h : h + 1], op0=ALU.mult, op1=ALU.mult)
 
-        def turn(x, g):
+        def turn(x, g, ts=range(4)):
             rec = st[x]
-            if g == 0:
+            if g == 0 and ts[0] == 0:
                 gr = grp.tile([P, NB, P, 4], BF16, tag="gr", align_bytes=64)
                 rec["gr"] = gr
-            at = pat.tile([P, 4, P], F32, tag="at")
-            rec["at%d" % g] = at
-            for t in range(4):
+            if ts[0] == 0:
+                at = pat.tile([P, 4, P], F32, tag="at")
+                rec["at%d" % g] = at
+            at = rec["at%d" % g]
+            for t in ts:
                 cols = slice((4 * g + t) * P, (4 * g + t + 1) * P)
                 nc.tensor.matmul(
                     at[:, t, :], lhsT=rec["sc0"][:, cols], rhs=ident_f[:], is_transpose=True, start=True, stop=False
@@ -342,10 +344,10 @@ def tile_differentialattention_kernel(tc, query, key, value, lambda_params, out)
                     rowmin(x, 0)
                 if s == 5 and live(x - 7) and x % 2 == 1:
                     finish(x - 7, 2)
-                if s % 2 == 1 and live(x - 3):
-                    g = s // 2
-                    turn(x - 3, g)
-                    copy_group(x - 3, g, "s")
+                if live(x - 3):
+                    turn(x - 3, s // 2, range(2 * (s % 2), 2 * (s % 2) + 2))
+                    if s % 2 == 1:
+                        copy_group(x - 3, s // 2, "s")
                 if s == 3 and live(x - 1):
                     expo(x - 1, 1)
             if x >= 1:

@@ -192,11 +192,11 @@ def tile_differentialattention_kernel(tc, query, key, value, lambda_params, out)
             nc.vector.reciprocal(out=rr[:], in_=rec["sm"][:])
             rec["rr"] = rr
 
-        def norm_half(x, c, eng):
+        def norm_maps(x, c0, c1, eng):
             h = x // NT
             rec = st[x]
             rr = rec["rr"]
-            cols = slice(c * HALF, (c + 1) * HALF)
+            cols = slice(c0, c1)
             a = rec["sc0"][:, cols]
             b = rec["sc1"][:, cols]
             eng.tensor_scalar(out=a, in0=a, scalar1=rr[:, 0:1], scalar2=0.0, op0=ALU.mult, op1=ALU.add)
@@ -241,7 +241,7 @@ def tile_differentialattention_kernel(tc, query, key, value, lambda_params, out)
         def pv(x):
             h = x // NT
             rec = st[x]
-            if x % 2 == 0 or x == TOTAL - 1:
+            if x % 2 == 0:
                 o2 = pso.tile([P, 2, D], F32, tag="o2")
                 rec["o2"] = o2
             else:
@@ -323,31 +323,32 @@ def tile_differentialattention_kernel(tc, query, key, value, lambda_params, out)
                     for u in FIRST[s]:
                         prep_unit(u[0], 0, u[1], u[2], "sv"[turns[0] % 2])
                         turns[0] += 1
-                if s == 7 and live(x - 4):
-                    pv(x - 4)
+                if s == 7 and live(x - 5):
+                    pv(x - 5)
                 score(x, s)
                 if s == 0 and live(x - 1):
                     rowmin(x - 1, 1)
                     expo(x - 1, 0)
                 if s == 2:
-                    if live(x - 4):
-                        quant(x - 4)
+                    if live(x - 5):
+                        quant(x - 5)
                     if live(x - 2):
                         recip(x - 2)
-                        norm_half(x - 2, 0, nc.gpsimd)
-                        norm_half(x - 2, 1, nc.gpsimd)
+                        norm_maps(x - 2, 0, S, nc.gpsimd)
                     if 3 <= x <= 6:
                         regroup_v(1, x - 3)
-                if s == 4 and live(x - 6) and x % 2 == 0:
-                    stats(x - 6, 2)
+                if s == 4 and live(x - 7) and x % 2 == 1:
+                    stats(x - 7, 2)
                 if s == 5:
                     rowmin(x, 0)
-                if s == 5 and live(x - 7) and x % 2 == 1:
-                    finish(x - 7, 2)
-                if live(x - 3):
-                    turn(x - 3, s // 2, range(2 * (s % 2), 2 * (s % 2) + 2))
+                if s == 5 and live(x - 8) and x % 2 == 0:
+                    finish(x - 8, 2)
+                y = x - 3 if s >= 4 else x - 4
+                if live(y):
+                    g = (s // 2 + 2) % 4
+                    turn(y, g, range(2 * (s % 2), 2 * (s % 2) + 2))
                     if s % 2 == 1:
-                        copy_group(x - 3, s // 2, "s")
+                        copy_group(y, g, "s")
                 if s == 3 and live(x - 1):
                     expo(x - 1, 1)
             if x >= 1:
@@ -360,51 +361,49 @@ def tile_differentialattention_kernel(tc, query, key, value, lambda_params, out)
                 quant_v(1)
 
         z = TOTAL - 1
+
+        def turn_and_copy(x, g, eng):
+            turn(x, g)
+            copy_group(x, g, eng)
+
         rowmin(z, 1)
         expo(z, 0)
         expo(z, 1)
-        stats(z - 5, 2)
-        turn(z - 2, 0)
-        copy_group(z - 2, 0, "v")
-        turn(z - 2, 1)
-        copy_group(z - 2, 1, "v")
-        quant(z - 3)
+        turn_and_copy(z - 3, 2, "v")
+        turn_and_copy(z - 3, 3, "v")
+        quant(z - 4)
         recip(z - 1)
-        norm_half(z - 1, 0, nc.vector)
-        norm_half(z - 1, 1, nc.gpsimd)
-        pv(z - 3)
-        for g in (2, 3):
-            turn(z - 2, g)
-            copy_group(z - 2, g, "v")
-        turn(z - 1, 0)
-        copy_group(z - 1, 0, "v")
-        turn(z - 1, 1)
-        copy_group(z - 1, 1, "v")
+        norm_maps(z - 1, 0, HALF, nc.vector)
+        pv(z - 4)
+        turn_and_copy(z - 2, 0, "v")
+        turn_and_copy(z - 2, 1, "v")
+        norm_maps(z - 1, HALF, S, nc.vector)
+        finish(z - 7, 2)
+        turn_and_copy(z - 2, 2, "s")
+        turn_and_copy(z - 2, 3, "s")
         recip(z)
-        norm_half(z, 0, nc.vector)
+        norm_maps(z, 0, HALF, nc.vector)
+        turn_and_copy(z - 1, 0, "s")
+        turn_and_copy(z - 1, 1, "s")
+        norm_maps(z, HALF, S, nc.vector)
+        stats(z - 5, 2)
+        quant(z - 3)
+        pv(z - 3)
+        turn_and_copy(z - 1, 2, "s")
+        turn_and_copy(z - 1, 3, "s")
         quant(z - 2)
-        norm_half(z, 1, nc.vector)
-        for g in (2, 3):
-            turn(z - 1, g)
-            copy_group(z - 1, g, "s")
         pv(z - 2)
+        turn_and_copy(z, 0, "v")
+        turn_and_copy(z, 1, "s")
         finish(z - 5, 2)
-        turn(z, 0)
-        copy_group(z, 0, "v")
-        turn(z, 1)
-        copy_group(z, 1, "s")
         quant(z - 1)
-        turn(z, 2)
-        copy_group(z, 2, "v")
-        turn(z, 3)
-        copy_group(z, 3, "s")
-        stats(z - 3, 2)
         pv(z - 1)
+        turn_and_copy(z, 2, "v")
+        turn_and_copy(z, 3, "s")
+        stats(z - 3, 2)
         quant(z, 0, 2)
         quant(z, 2, 2)
-        stats(z - 1, 1)
-        finish(z - 3, 2)
         pv(z)
-        stats(z, 1)
-        finish(z - 1, 1)
-        finish(z, 1)
+        finish(z - 3, 2)
+        stats(z - 1, 2)
+        finish(z - 1, 2)

@@ -83,6 +83,11 @@ def tile_differentialattention_kernel(tc, query, key, value, lambda_params, out)
         make_identity(nc, ident_bf[:])
         ident_f = const.tile([P, P], F32, name="ident_f")
         make_identity(nc, ident_f[:])
+        zero = const.tile([P, 512], BF16, name="zero")
+        nc.vector.memset(zero[:], 0.0)
+        wps = pso.tile([P, 512], F32, tag="o2")
+        for k in range(6):
+            nc.tensor.matmul(wps[:], lhsT=zero[:, 0:P], rhs=zero[:], start=True, stop=True)
         mhalf = const.tile([P, 2], F32, name="mhalf")
         nc.vector.memset(mhalf[:], -0.5)
         warm = const.tile([P, 1], F32, name="warm")
@@ -121,10 +126,10 @@ def tile_differentialattention_kernel(tc, query, key, value, lambda_params, out)
                 nc.tensor.transpose(pt[:, a, :], src[:, m * P : (m + 1) * P], ident_bf[:])
             copy(eng, dst[:, n0 * P : (n0 + 4) * P], pt[:].rearrange("p a q -> p (a q)"))
 
-        def regroup_v(h, g):
+        def regroup_v(h, g, d0=0, d1=D):
             nc.gpsimd.tensor_scalar(
-                out=vgrp[h][:, g],
-                in0=vraw[h][:, g].rearrange("p t d -> p d t"),
+                out=vgrp[h][:, g, d0:d1],
+                in0=vraw[h][:, g, :, d0:d1].rearrange("p t d -> p d t"),
                 scalar1=1.0,
                 scalar2=0.0,
                 op0=ALU.mult,
@@ -202,13 +207,13 @@ def tile_differentialattention_kernel(tc, query, key, value, lambda_params, out)
             eng.tensor_scalar(out=a, in0=a, scalar1=rr[:, 0:1], scalar2=0.0, op0=ALU.mult, op1=ALU.add)
             eng.tensor_scalar(out=b, in0=b, scalar1=rr[:, 1:2], scalar2=neglam[:, h : h + 1], op0=ALU.mult, op1=ALU.mult)
 
-        def turn(x, g, ts=range(4)):
+        def turn(x, g, ts=range(4), pool=pat, tag="at"):
             rec = st[x]
             if g == 0 and ts[0] == 0:
                 gr = grp.tile([P, NB, P, 4], BF16, tag="gr", align_bytes=64)
                 rec["gr"] = gr
             if ts[0] == 0:
-                at = pat.tile([P, 4, P], F32, tag="at")
+                at = pool.tile([P, 4, P], F32, tag=tag)
                 rec["at%d" % g] = at
             at = rec["at%d" % g]
             for t in ts:
@@ -335,8 +340,9 @@ def tile_differentialattention_kernel(tc, query, key, value, lambda_params, out)
                     if live(x - 2):
                         recip(x - 2)
                         norm_maps(x - 2, 0, S, nc.gpsimd)
-                    if 3 <= x <= 6:
-                        regroup_v(1, x - 3)
+                    if x % 2 == 0 and 4 <= x <= 18:
+                        k = (x - 4) // 2
+                        regroup_v(1, k // 2, (k % 2) * P, (k % 2 + 1) * P)
                 if s == 4 and live(x - 7) and x % 2 == 1:
                     stats(x - 7, 2)
                 if s == 5:
@@ -348,7 +354,8 @@ def tile_differentialattention_kernel(tc, query, key, value, lambda_params, out)
                     g = (s // 2 + 2) % 4
                     turn(y, g, range(2 * (s % 2), 2 * (s % 2) + 2))
                     if s % 2 == 1:
-                        copy_group(y, g, "s")
+                        if x < TOTAL - 1 or s < 4:
+                            copy_group(y, g, "s")
                 if s == 3 and live(x - 1):
                     expo(x - 1, 1)
             if x >= 1:
@@ -357,53 +364,134 @@ def tile_differentialattention_kernel(tc, query, key, value, lambda_params, out)
                     next_unit()
             if x == 2:
                 quant_v(0)
-            if x == 8:
+            if x == 19:
                 quant_v(1)
 
         z = TOTAL - 1
+        dummy = psc.tile([P, 512], F32, tag="ps")
+        flip = [0]
 
-        def turn_and_copy(x, g, eng):
-            turn(x, g)
+        def tc2(x, g, eng, keep_warm=True):
+            flip[0] += 1
+            if flip[0] % 2:
+                turn(x, g, pool=psc, tag="ps")
+            else:
+                turn(x, g)
             copy_group(x, g, eng)
+            if keep_warm:
+                nc.tensor.matmul(dummy[:], lhsT=qT[(1, 0)][:, 0:P], rhs=kT[(1, 0)][:, 0:512], start=True, stop=True)
+
+        def recip_map(x, m):
+            rec = st[x]
+            if m == 0:
+                rr = small.tile([P, 2], F32, tag="rr")
+                rec["rr"] = rr
+            nc.vector.reciprocal(out=rec["rr"][:, m : m + 1], in_=rec["sm"][:, m : m + 1])
+            if m == 1:
+                nl = small.tile([P, 1], F32, tag="nl")
+                nc.vector.tensor_scalar(
+                    out=nl[:], in0=rec["rr"][:, 1:2], scalar1=neglam[:, x // NT : x // NT + 1], scalar2=None, op0=ALU.mult
+                )
+                rec["nl"] = nl
+
+        def norm0(x, c0, c1):
+            rec = st[x]
+            a = rec["sc0"][:, c0:c1]
+            nc.vector.tensor_scalar(out=a, in0=a, scalar1=rec["rr"][:, 0:1], scalar2=None, op0=ALU.mult)
+
+        def combine(x, c0, c1):
+            rec = st[x]
+            if c0 == 0:
+                cb = grp.tile([P, S], BF16, tag="cb")
+                rec["cb"] = cb
+            nc.vector.scalar_tensor_tensor(
+                out=rec["cb"][:, c0:c1],
+                in0=rec["sc1"][:, c0:c1],
+                scalar=rec["nl"][:],
+                in1=rec["sc0"][:, c0:c1],
+                op0=ALU.mult,
+                op1=ALU.add,
+            )
+
+        def tb(x, g, eng):
+            rec = st[x]
+            if g == 0:
+                gr = grp.tile([P, NB, P, 4], BF16, tag="gr", align_bytes=64)
+                rec["gr"] = gr
+            flip[0] += 1
+            pool, tag = (psc, "ps") if flip[0] % 2 else (pat, "at")
+            at = pool.tile([P, 4, P], BF16, tag=tag)
+            rec["at%d" % g] = at
+            for t in range(4):
+                nc.tensor.transpose(at[:, t, :], rec["cb"][:, (4 * g + t) * P : (4 * g + t + 1) * P], ident_bf[:])
+            copy_group(x, g, eng)
+
+        def finish2(x0, eng0, eng1):
+            h, i = divmod(x0, NT)
+            rec = st[x0]
+            nb = small.tile([P, 2], F32, tag="nb")
+            for k in range(2):
+                nc.gpsimd.tensor_scalar(
+                    out=nb[:, k : k + 1], in0=rec["mv"][:, k, 0:1], scalar1=rec["rs"][:, k : k + 1], scalar2=-1.0, op0=ALU.mult, op1=ALU.mult
+                )
+            res = outp.tile([P, 2, D], F32, tag="res")
+            for k in range(2):
+                o = st[x0 + k]["o2"][:, (x0 + k) % 2, :]
+                if (eng0, eng1)[k] == "s":
+                    nc.scalar.activation(
+                        out=res[:, k, :], in_=o, func=ACT.Identity, bias=nb[:, k : k + 1], scale=rec["rs"][:, k : k + 1]
+                    )
+                else:
+                    nc.vector.tensor_scalar(
+                        out=res[:, k, :], in0=o, scalar1=rec["mv"][:, k, 0:1], scalar2=rec["rs"][:, k : k + 1], op0=ALU.subtract, op1=ALU.mult
+                    )
+            nc.sync.dma_start(
+                out=out[0, h, i * P : (i + 2) * P, :].rearrange("(n p) d -> p n d", p=P), in_=res[:]
+            )
 
         rowmin(z, 1)
         expo(z, 0)
         expo(z, 1)
-        turn_and_copy(z - 3, 2, "v")
-        turn_and_copy(z - 3, 3, "v")
+        copy_group(z - 3, 0, "s")
+        copy_group(z - 3, 1, "s")
+        tc2(z - 3, 2, "s")
+        tc2(z - 3, 3, "s")
         quant(z - 4)
-        recip(z - 1)
-        norm_maps(z - 1, 0, HALF, nc.vector)
+        recip_map(z - 1, 0)
+        recip_map(z - 1, 1)
+        norm0(z - 1, 0, S)
+        combine(z - 1, 0, HALF)
+        tc2(z - 2, 0, "s", False)
         pv(z - 4)
-        turn_and_copy(z - 2, 0, "v")
-        turn_and_copy(z - 2, 1, "v")
-        norm_maps(z - 1, HALF, S, nc.vector)
-        finish(z - 7, 2)
-        turn_and_copy(z - 2, 2, "s")
-        turn_and_copy(z - 2, 3, "s")
-        recip(z)
-        norm_maps(z, 0, HALF, nc.vector)
-        turn_and_copy(z - 1, 0, "s")
-        turn_and_copy(z - 1, 1, "s")
-        norm_maps(z, HALF, S, nc.vector)
-        stats(z - 5, 2)
+        tc2(z - 2, 1, "s", False)
+        combine(z - 1, HALF, S)
+        recip_map(z, 0)
+        norm0(z, 0, S)
+        tb(z - 1, 0, "v")
+        tb(z - 1, 1, "v")
+        recip_map(z, 1)
+        combine(z, 0, HALF)
+        combine(z, HALF, S)
+        tc2(z - 2, 2, "s", False)
+        tc2(z - 2, 3, "s", False)
+        tb(z - 1, 2, "s")
+        tb(z - 1, 3, "s")
         quant(z - 3)
-        pv(z - 3)
-        turn_and_copy(z - 1, 2, "s")
-        turn_and_copy(z - 1, 3, "s")
+        stats(z - 5, 2)
+        tb(z, 0, "s")
+        tb(z, 1, "s")
         quant(z - 2)
-        pv(z - 2)
-        turn_and_copy(z, 0, "v")
-        turn_and_copy(z, 1, "s")
-        finish(z - 5, 2)
+        pv(z - 3)
+        finish2(z - 7, "s", "s")
+        tb(z, 2, "s")
+        tb(z, 3, "s")
         quant(z - 1)
+        finish2(z - 5, "s", "s")
+        pv(z - 2)
+        quant(z)
         pv(z - 1)
-        turn_and_copy(z, 2, "v")
-        turn_and_copy(z, 3, "s")
-        stats(z - 3, 2)
-        quant(z, 0, 2)
-        quant(z, 2, 2)
         pv(z)
-        finish(z - 3, 2)
+        stats(z - 3, 2)
         stats(z - 1, 2)
-        finish(z - 1, 2)
+        finish2(z - 3, "s", "s")
+        finish2(z - 1, "v", "s")

@@ -45,7 +45,8 @@ def tile_differentialattention_kernel(tc, query, key, value, lambda_params, out)
         raw = ctx.enter_context(tc.tile_pool(name="raw", bufs=2))
         keep = ctx.enter_context(tc.tile_pool(name="keep", bufs=1))
         work = ctx.enter_context(tc.tile_pool(name="work", bufs=5))
-        grp = ctx.enter_context(tc.tile_pool(name="grp", bufs=3))
+        grp = ctx.enter_context(tc.tile_pool(name="grp", bufs=4))
+        comb = ctx.enter_context(tc.tile_pool(name="comb", bufs=2))
         small = ctx.enter_context(tc.tile_pool(name="small", bufs=6))
         outp = ctx.enter_context(tc.tile_pool(name="outp", bufs=3))
         psc = ctx.enter_context(tc.psum_pool(name="psc", bufs=3))
@@ -243,11 +244,11 @@ def tile_differentialattention_kernel(tc, query, key, value, lambda_params, out)
                 in_=rec["gr"][:, g0 : g0 + n].rearrange("p g q t -> p (g q t)"),
             )
 
-        def pv(x):
+        def pv(x, pool=pso, tag="o2"):
             h = x // NT
             rec = st[x]
             if x % 2 == 0:
-                o2 = pso.tile([P, 2, D], F32, tag="o2")
+                o2 = pool.tile([P, 2, D], F32, tag=tag)
                 rec["o2"] = o2
             else:
                 rec["o2"] = st[x - 1]["o2"]
@@ -328,13 +329,13 @@ def tile_differentialattention_kernel(tc, query, key, value, lambda_params, out)
                     for u in FIRST[s]:
                         prep_unit(u[0], 0, u[1], u[2], "sv"[turns[0] % 2])
                         turns[0] += 1
-                if s == 7 and live(x - 5):
+                if s == 6 and live(x - 5):
                     pv(x - 5)
                 score(x, s)
                 if s == 0 and live(x - 1):
                     rowmin(x - 1, 1)
                     expo(x - 1, 0)
-                if s == 2:
+                if s == 1:
                     if live(x - 5):
                         quant(x - 5)
                     if live(x - 2):
@@ -402,7 +403,7 @@ def tile_differentialattention_kernel(tc, query, key, value, lambda_params, out)
         def combine(x, c0, c1):
             rec = st[x]
             if c0 == 0:
-                cb = grp.tile([P, S], BF16, tag="cb")
+                cb = comb.tile([P, S], BF16, tag="cb")
                 rec["cb"] = cb
             nc.vector.scalar_tensor_tensor(
                 out=rec["cb"][:, c0:c1],
@@ -471,27 +472,27 @@ def tile_differentialattention_kernel(tc, query, key, value, lambda_params, out)
         tb(z - 1, 1, "v")
         recip_map(z, 1)
         combine(z, 0, HALF)
-        combine(z, HALF, S)
         tc2(z - 2, 2, "s", False)
         tc2(z - 2, 3, "s", False)
+        combine(z, HALF, S)
+        finish2(z - 7, "s", "s")
         tb(z - 1, 2, "s")
         tb(z - 1, 3, "s")
-        quant(z - 3)
-        stats(z - 5, 2)
         tb(z, 0, "s")
         tb(z, 1, "s")
-        quant(z - 2)
-        pv(z - 3)
-        finish2(z - 7, "s", "s")
         tb(z, 2, "s")
         tb(z, 3, "s")
-        quant(z - 1)
-        finish2(z - 5, "s", "s")
+        quant(z - 3)
+        pv(z - 3)
+        quant(z - 2)
         pv(z - 2)
+        quant(z - 1)
+        pv(z - 1, psc, "ps")
+        stats(z - 5, 2)
         quant(z)
-        pv(z - 1)
         pv(z)
+        finish2(z - 5, "s", "s")
         stats(z - 3, 2)
         stats(z - 1, 2)
-        finish2(z - 3, "s", "s")
+        finish2(z - 3, "v", "v")
         finish2(z - 1, "v", "s")

@@ -244,10 +244,10 @@ def tile_differentialattention_kernel(tc, query, key, value, lambda_params, out)
                 in_=rec["gr"][:, g0 : g0 + n].rearrange("p g q t -> p (g q t)"),
             )
 
-        def pv(x, pool=pso, tag="o2"):
+        def pv(x, pool=pso, tag="o2", fresh=False):
             h = x // NT
             rec = st[x]
-            if x % 2 == 0:
+            if x % 2 == 0 or fresh:
                 o2 = pool.tile([P, 2, D], F32, tag=tag)
                 rec["o2"] = o2
             else:
@@ -432,6 +432,8 @@ def tile_differentialattention_kernel(tc, query, key, value, lambda_params, out)
             rec = st[x0]
             nb = small.tile([P, 2], F32, tag="nb")
             for k in range(2):
+                if (eng0, eng1)[k] == "v":
+                    continue
                 nc.gpsimd.tensor_scalar(
                     out=nb[:, k : k + 1], in0=rec["mv"][:, k, 0:1], scalar1=rec["rs"][:, k : k + 1], scalar2=-1.0, op0=ALU.mult, op1=ALU.mult
                 )
@@ -450,11 +452,16 @@ def tile_differentialattention_kernel(tc, query, key, value, lambda_params, out)
                 out=out[0, h, i * P : (i + 2) * P, :].rearrange("(n p) d -> p n d", p=P), in_=res[:]
             )
 
+        def norm0s(x, c0, c1):
+            rec = st[x]
+            a = rec["sc0"][:, c0:c1]
+            nc.scalar.activation(out=a, in_=a, func=ACT.Copy, scale=rec["rr"][:, 0:1])
+
         rowmin(z, 1)
         expo(z, 0)
         expo(z, 1)
-        copy_group(z - 3, 0, "s")
-        copy_group(z - 3, 1, "s")
+        copy_group(z - 3, 0, "v")
+        copy_group(z - 3, 1, "v")
         tc2(z - 3, 2, "s")
         tc2(z - 3, 3, "s")
         quant(z - 4)
@@ -468,8 +475,8 @@ def tile_differentialattention_kernel(tc, query, key, value, lambda_params, out)
         combine(z - 1, HALF, S)
         recip_map(z, 0)
         norm0(z, 0, S)
-        tb(z - 1, 0, "v")
-        tb(z - 1, 1, "v")
+        tb(z - 1, 0, "s")
+        tb(z - 1, 1, "s")
         recip_map(z, 1)
         combine(z, 0, HALF)
         tc2(z - 2, 2, "s", False)
@@ -490,7 +497,7 @@ def tile_differentialattention_kernel(tc, query, key, value, lambda_params, out)
         pv(z - 1, psc, "ps")
         stats(z - 5, 2)
         quant(z)
-        pv(z)
+        pv(z, pat, "at", True)
         finish2(z - 5, "s", "s")
         stats(z - 3, 2)
         stats(z - 1, 2)

import math
from contextlib import ExitStack

import concourse.mybir as mybir
from concourse.masks import make_identity

F32 = mybir.dt.float32
BF16 = mybir.dt.bfloat16
U32 = mybir.dt.uint32
U8 = mybir.dt.uint8
FP8X4 = mybir.dt.float8_e4m3fn_x4
ALU = mybir.AluOpType
ACT = mybir.ActivationFunctionType
AX = mybir.AxisListType

P = 128
H = 2
S = 2048
D = 256
D2 = 128
NT = S // P
NB = S // 512
HALF = S // 2
SCALE = 1.0 / math.sqrt(D2)
EPS = 1e-5
GAIN = 0.2
FLOPS = H * (2 * 2 * S * S * D2 + 2 * S * S * D)
TOTAL = H * NT
FIRST = (
    (("k", 0, 0), ("q", 0, 0), ("k", 4, 0)),
    (("k", 8, 0),),
    (("k", 12, 0),),
    (("k", 0, 1), ("q", 0, 1)),
    (("k", 4, 1),),
    (("k", 8, 1),),
    (("k", 12, 1),),
    (),
)


def tile_differentialattention_kernel(tc, query, key, value, lambda_params, out):
    nc = tc.nc
    with ExitStack() as ctx:
        const = ctx.enter_context(tc.tile_pool(name="const", bufs=1))
        raw = ctx.enter_context(tc.tile_pool(name="raw", bufs=2))
        keep = ctx.enter_context(tc.tile_pool(name="keep", bufs=1))
        work = ctx.enter_context(tc.tile_pool(name="work", bufs=5))
        grp = ctx.enter_context(tc.tile_pool(name="grp", bufs=4))
        comb = ctx.enter_context(tc.tile_pool(name="comb", bufs=2))
        small = ctx.enter_context(tc.tile_pool(name="small", bufs=6))
        outp = ctx.enter_context(tc.tile_pool(name="outp", bufs=3))
        psc = ctx.enter_context(tc.psum_pool(name="psc", bufs=3))
        pat = ctx.enter_context(tc.psum_pool(name="pat", bufs=3))
        pso = ctx.enter_context(tc.psum_pool(name="pso", bufs=2))
        ctx.enter_context(tc.manual_schedule())

        lam_bf = const.tile([P, H], BF16, name="lam_bf")
        kraw = {}
        qraw = {}
        vraw = {}
        views = {}
        for h in range(H):
            kr = raw.tile([P, NB, 4, D], BF16, tag="kraw")
            qr = raw.tile([P, NT, D], BF16, tag="qraw")
            vr = raw.tile([P, NB, 4, D], BF16, tag="vraw")
            kraw[h] = kr
            qraw[h] = qr
            vraw[h] = vr
            views[("k", h)] = key[0, h].rearrange("(g p t) d -> p g t d", p=P, t=4)
            views[("q", h)] = query[0, h].rearrange("(n p) d -> p n d", p=P)
            views[("v", h)] = value[0, h].rearrange("(g p t) d -> p g t d", p=P, t=4)
        nc.sync.dma_start(out=kraw[0][:, 0], in_=views[("k", 0)][:, 0])
        nc.sync.dma_start(out=qraw[0][:, 0:4, :], in_=views[("q", 0)][:, 0:4, :])
        for c in range(1, 4):
            nc.sync.dma_start(out=kraw[0][:, c], in_=views[("k", 0)][:, c])
        nc.sync.dma_start(out=lam_bf[:], in_=lambda_params.partition_broadcast(P))
        nc.sync.dma_start(out=vraw[0][:], in_=views[("v", 0)])
        nc.sync.dma_start(out=qraw[0][:, 4:16, :], in_=views[("q", 0)][:, 4:16, :])
        nc.sync.dma_start(out=kraw[1][:], in_=views[("k", 1)])
        nc.sync.dma_start(out=qraw[1][:], in_=views[("q", 1)])
        nc.sync.dma_start(out=vraw[1][:], in_=views[("v", 1)])

        ident_bf = const.tile([P, P], BF16, name="ident_bf")
        make_identity(nc, ident_bf[:])
        ident_f = const.tile([P, P], F32, name="ident_f")
        make_identity(nc, ident_f[:])
        zero = const.tile([P, 512], BF16, name="zero")
        nc.vector.memset(zero[:], 0.0)
        wps = pso.tile([P, 512], F32, tag="o2")
        for k in range(6):
            nc.tensor.matmul(wps[:], lhsT=zero[:, 0:P], rhs=zero[:], start=True, stop=True)
        mhalf = const.tile([P, 2], F32, name="mhalf")
        nc.vector.memset(mhalf[:], -0.5)
        warm = const.tile([P, 1], F32, name="warm")
        nc.scalar.activation(out=warm[:], in_=mhalf[:, 0:1], func=ACT.Exp)
        neglam = const.tile([P, H], F32, name="neglam")

        qT = {}
        kT = {}
        vcod = {}
        vpl = {}
        vgrp = {}
        for h in range(H):
            for m in range(2):
                a = keep.tile([P, S], BF16, name="qT%d%d" % (h, m))
                b = keep.tile([P, S], BF16, name="kT%d%d" % (h, m))
                qT[(h, m)] = a
                kT[(h, m)] = b
            c = keep.tile([P, NB, D], U32, name="vcod%d" % h, align_bytes=64)
            d = keep.tile([P, NB, D], U8, name="vpl%d" % h, align_bytes=64)
            e = keep.tile([P, NB, D, 4], BF16, name="vgrp%d" % h, align_bytes=64)
            vcod[h] = c
            vpl[h] = d
            vgrp[h] = e

        def copy(eng, dst, src):
            if eng == "s":
                nc.scalar.copy(out=dst, in_=src)
            else:
                nc.vector.tensor_copy(out=dst, in_=src)

        def prep_unit(kind, h, n0, m, eng):
            dst = kT[(h, m)] if kind == "k" else qT[(h, m)]
            pt = pat.tile([P, 4, P], BF16, tag="at")
            for a in range(4):
                src = kraw[h][:, n0 // 4, a] if kind == "k" else qraw[h][:, n0 + a]
                nc.tensor.transpose(pt[:, a, :], src[:, m * P : (m + 1) * P], ident_bf[:])
            copy(eng, dst[:, n0 * P : (n0 + 4) * P], pt[:].rearrange("p a q -> p (a q)"))

        def regroup_v(h, g, d0=0, d1=D):
            nc.gpsimd.tensor_scalar(
                out=vgrp[h][:, g, d0:d1],
                in0=vraw[h][:, g, :, d0:d1].rearrange("p t d -> p d t"),
                scalar1=1.0,
                scalar2=0.0,
                op0=ALU.mult,
                op1=ALU.add,
            )

        def quant_v(h):
            nc.vector.quantize_mx(
                out=vcod[h][:].rearrange("p g d -> p (g d)").bitcast(FP8X4),
                scales=vpl[h][:].rearrange("p g d -> p (g d)"),
                in_=vgrp[h][:].rearrange("p g d t -> p (g d t)"),
            )

        st = {}

        def live(x):
            return 0 <= x < TOTAL

        def score(x, s):
            h, i = divmod(x, NT)
            m, j = divmod(s, NB)
            if s == 0:
                sm = small.tile([P, 2], F32, tag="sm")
                st[x] = {"sm": sm}
            rec = st[x]
            if j == 0:
                sc = work.tile([P, S], F32, tag="sc%d" % m)
                mn = small.tile([P, NB], F32, tag="mn%d" % m)
                rec["sc%d" % m] = sc
                rec["mn%d" % m] = mn
            ps = psc.tile([P, 512], F32, tag="ps")
            nc.tensor.matmul(
                ps[:],
                lhsT=qT[(h, m)][:, i * P : (i + 1) * P],
                rhs=kT[(h, m)][:, j * 512 : (j + 1) * 512],
                start=True,
                stop=True,
            )
            nc.vector.tensor_scalar(
                out=rec["sc%d" % m][:, j * 512 : (j + 1) * 512],
                in0=ps[:],
                scalar1=-SCALE,
                scalar2=None,
                op0=ALU.mult,
                op1=ALU.min,
                accum_out=rec["mn%d" % m][:, j : j + 1],
            )

        def rowmin(x, m):
            rec = st[x]
            nm = small.tile([P, 1], F32, tag="nm%d" % m)
            nc.vector.tensor_reduce(out=nm[:], in_=rec["mn%d" % m][:], axis=AX.X, op=ALU.min)
            rec["nm%d" % m] = nm

        def expo(x, m):
            rec = st[x]
            sc = rec["sc%d" % m]
            nc.scalar.activation(
                out=sc[:], in_=sc[:], func=ACT.Exp, bias=rec["nm%d" % m][:], scale=-1.0, accum_out=rec["sm"][:, m : m + 1]
            )

        def recip(x):
            rec = st[x]
            rr = small.tile([P, 2], F32, tag="rr")
            nc.vector.reciprocal(out=rr[:], in_=rec["sm"][:])
            rec["rr"] = rr

        def norm_maps(x, c0, c1, eng):
            h = x // NT
            rec = st[x]
            rr = rec["rr"]
            cols = slice(c0, c1)
            a = rec["sc0"][:, cols]
            b = rec["sc1"][:, cols]
            eng.tensor_scalar(out=a, in0=a, scalar1=rr[:, 0:1], scalar2=0.0, op0=ALU.mult, op1=ALU.add)
            eng.tensor_scalar(out=b, in0=b, scalar1=rr[:, 1:2], scalar2=neglam[:, h : h + 1], op0=ALU.mult, op1=ALU.mult)

        def turn(x, g, ts=range(4), pool=pat, tag="at"):
            rec = st[x]
            if g == 0 and ts[0] == 0:
                gr = grp.tile([P, NB, P, 4], BF16, tag="gr", align_bytes=64)
                rec["gr"] = gr
            if ts[0] == 0:
                at = pool.tile([P, 4, P], F32, tag=tag)
                rec["at%d" % g] = at
            at = rec["at%d" % g]
            for t in ts:
                cols = slice((4 * g + t) * P, (4 * g + t + 1) * P)
                nc.tensor.matmul(
                    at[:, t, :], lhsT=rec["sc0"][:, cols], rhs=ident_f[:], is_transpose=True, start=True, stop=False
                )
                nc.tensor.matmul(
                    at[:, t, :], lhsT=rec["sc1"][:, cols], rhs=ident_f[:], is_transpose=True, start=False, stop=True
                )

        def copy_group(x, g, eng):
            rec = st[x]
            copy(eng, rec["gr"][:, g], rec["at%d" % g][:].rearrange("p t q -> p q t"))

        def quant(x, g0=0, n=NB):
            rec = st[x]
            if g0 == 0:
                cod = grp.tile([P, NB * P], U32, tag="cod", align_bytes=64)
                pl = grp.tile([P, NB * P], U8, tag="pl", align_bytes=64)
                rec["cod"] = cod
                rec["pl"] = pl
            cols = slice(g0 * P, (g0 + n) * P)
            nc.vector.quantize_mx(
                out=rec["cod"][:, cols].bitcast(FP8X4),
                scales=rec["pl"][:, cols],
                in_=rec["gr"][:, g0 : g0 + n].rearrange("p g q t -> p (g q t)"),
            )

        def pv(x, pool=pso, tag="o2", fresh=False):
            h = x // NT
            rec = st[x]
            if x % 2 == 0 or fresh:
                o2 = pool.tile([P, 2, D], F32, tag=tag)
                rec["o2"] = o2
            else:
                rec["o2"] = st[x - 1]["o2"]
            for g in range(NB):
                nc.tensor.matmul_mx(
                    out=rec["o2"][:, x % 2, :],
                    lhsT=rec["cod"][:, g * P : (g + 1) * P].bitcast(FP8X4),
                    lhsT_scale=rec["pl"][:, g * P : (g + 1) * P],
                    rhs=vcod[h][:, g, :].bitcast(FP8X4),
                    rhs_scale=vpl[h][:, g, :],
                    start=(g == 0),
                    stop=(g == NB - 1),
                )

        def stats(x0, n):
            rec = st[x0]
            bs = small.tile([P, 2, 6], F32, tag="bs")
            mv = small.tile([P, 2, 2], F32, tag="mv")
            for k in range(n):
                nc.vector.bn_stats(out=bs[:, k, :], in_=st[x0 + k]["o2"][:, (x0 + k) % 2, :])
            for k in range(n):
                nc.vector.bn_aggr(out=mv[:, k, :], in_=bs[:, k, :])
            v25 = small.tile([P, 2], F32, tag="v25")
            nc.gpsimd.tensor_scalar(
                out=v25[:, 0:n],
                in0=mv[:, 0:n, 1],
                scalar1=1.0 / (GAIN * GAIN),
                scalar2=EPS / (GAIN * GAIN),
                op0=ALU.mult,
                op1=ALU.add,
            )
            rs = small.tile([P, 2], F32, tag="rs")
            nc.gpsimd.tensor_tensor(out=rs[:, 0:n], in0=v25[:, 0:n], in1=mhalf[:, 0:n], op=ALU.pow)
            rec["mv"] = mv
            rec["rs"] = rs

        def finish(x0, n):
            h, i = divmod(x0, NT)
            rec = st[x0]
            res = outp.tile([P, 2, D], F32, tag="res")
            for k in range(n):
                nc.vector.tensor_scalar(
                    out=res[:, k, :],
                    in0=st[x0 + k]["o2"][:, (x0 + k) % 2, :],
                    scalar1=rec["mv"][:, k, 0:1],
                    scalar2=rec["rs"][:, k : k + 1],
                    op0=ALU.subtract,
                    op1=ALU.mult,
                )
            nc.sync.dma_start(
                out=out[0, h, i * P : (i + n) * P, :].rearrange("(n p) d -> p n d", p=P), in_=res[:, 0:n, :]
            )

        later = []
        for n0 in (4, 8, 12):
            for m in range(2):
                later.append(("q", 0, n0, m))
        for kind in ("k", "q"):
            for n0 in (0, 4, 8, 12):
                for m in range(2):
                    later.append((kind, 1, n0, m))
        pos = [0]

        def next_unit():
            if pos[0] < len(later):
                u = later[pos[0]]
                pos[0] += 1
                prep_unit(u[0], u[1], u[2], u[3], "v")

        nc.gpsimd.tensor_scalar(out=neglam[:], in0=lam_bf[:], scalar1=-1.0, scalar2=0.0, op0=ALU.mult, op1=ALU.add)
        for g in range(NB):
            regroup_v(0, g)

        turns = [0]
        for x in range(TOTAL):
            for s in range(8):
                if x == 0:
                    for u in FIRST[s]:
                        prep_unit(u[0], 0, u[1], u[2], "sv"[turns[0] % 2])
                        turns[0] += 1
                if s == 6 and live(x - 5):
                    pv(x - 5)
                score(x, s)
                if s == 0 and live(x - 1):
                    rowmin(x - 1, 1)
                    expo(x - 1, 0)
                if s == 1:
                    if live(x - 5):
                        quant(x - 5)
                    if live(x - 2):
                        recip(x - 2)
                        norm_maps(x - 2, 0, S, nc.gpsimd)
                    if x % 2 == 0 and 4 <= x <= 18:
                        k = (x - 4) // 2
                        regroup_v(1, k // 2, (k % 2) * P, (k % 2 + 1) * P)
                if s == 4 and live(x - 7) and x % 2 == 1:
                    stats(x - 7, 2)
                if s == 5:
                    rowmin(x, 0)
                if s == 5 and live(x - 8) and x % 2 == 0:
                    finish(x - 8, 2)
                y = x - 3 if s >= 4 else x - 4
                if live(y):
                    g = (s // 2 + 2) % 4
                    turn(y, g, range(2 * (s % 2), 2 * (s % 2) + 2))
                    if s % 2 == 1:
                        if x < TOTAL - 1 or s < 4:
                            copy_group(y, g, "s")
                if s == 3 and live(x - 1):
                    expo(x - 1, 1)
            if x >= 1:
                next_unit()
                if x <= 3:
                    next_unit()
            if x == 2:
                quant_v(0)
            if x == 19:
                quant_v(1)

        z = TOTAL - 1
        dummy = psc.tile([P, 512], F32, tag="ps")
        flip = [0]

        def tc2(x, g, eng, keep_warm=True):
            flip[0] += 1
            if flip[0] % 2:
                turn(x, g, pool=psc, tag="ps")
            else:
                turn(x, g)
            copy_group(x, g, eng)
            if keep_warm:
                nc.tensor.matmul(dummy[:], lhsT=qT[(1, 0)][:, 0:P], rhs=kT[(1, 0)][:, 0:512], start=True, stop=True)

        def recip_map(x, m):
            rec = st[x]
            if m == 0:
                rr = small.tile([P, 2], F32, tag="rr")
                rec["rr"] = rr
            nc.vector.reciprocal(out=rec["rr"][:, m : m + 1], in_=rec["sm"][:, m : m + 1])
            if m == 1:
                nl = small.tile([P, 1], F32, tag="nl")
                nc.vector.tensor_scalar(
                    out=nl[:], in0=rec["rr"][:, 1:2], scalar1=neglam[:, x // NT : x // NT + 1], scalar2=None, op0=ALU.mult
                )
                rec["nl"] = nl

        def norm0(x, c0, c1):
            rec = st[x]
            a = rec["sc0"][:, c0:c1]
            nc.vector.tensor_scalar(out=a, in0=a, scalar1=rec["rr"][:, 0:1], scalar2=None, op0=ALU.mult)

        def combine(x, c0, c1):
            rec = st[x]
            if c0 == 0:
                cb = comb.tile([P, S], BF16, tag="cb")
                rec["cb"] = cb
            nc.vector.scalar_tensor_tensor(
                out=rec["cb"][:, c0:c1],
                in0=rec["sc1"][:, c0:c1],
                scalar=rec["nl"][:],
                in1=rec["sc0"][:, c0:c1],
                op0=ALU.mult,
                op1=ALU.add,
            )

        def tb(x, g, eng):
            rec = st[x]
            if g == 0:
                gr = grp.tile([P, NB, P, 4], BF16, tag="gr", align_bytes=64)
                rec["gr"] = gr
            flip[0] += 1
            pool, tag = (psc, "ps") if flip[0] % 2 else (pat, "at")
            at = pool.tile([P, 4, P], BF16, tag=tag)
            rec["at%d" % g] = at
            for t in range(4):
                nc.tensor.transpose(at[:, t, :], rec["cb"][:, (4 * g + t) * P : (4 * g + t + 1) * P], ident_bf[:])
            copy_group(x, g, eng)

        def finish2(x0, eng0, eng1):
            h, i = divmod(x0, NT)
            rec = st[x0]
            nb = small.tile([P, 2], F32, tag="nb")
            for k in range(2):
                if (eng0, eng1)[k] == "v":
                    continue
                nc.gpsimd.tensor_scalar(
                    out=nb[:, k : k + 1], in0=rec["mv"][:, k, 0:1], scalar1=rec["rs"][:, k : k + 1], scalar2=-1.0, op0=ALU.mult, op1=ALU.mult
                )
            res = outp.tile([P, 2, D], F32, tag="res")
            for k in range(2):
                o = st[x0 + k]["o2"][:, (x0 + k) % 2, :]
                if (eng0, eng1)[k] == "s":
                    nc.scalar.activation(
                        out=res[:, k, :], in_=o, func=ACT.Identity, bias=nb[:, k : k + 1], scale=rec["rs"][:, k : k + 1]
                    )
                else:
                    nc.vector.tensor_scalar(
                        out=res[:, k, :], in0=o, scalar1=rec["mv"][:, k, 0:1], scalar2=rec["rs"][:, k : k + 1], op0=ALU.subtract, op1=ALU.mult
                    )
            nc.sync.dma_start(
                out=out[0, h, i * P : (i + 2) * P, :].rearrange("(n p) d -> p n d", p=P), in_=res[:]
            )

        def norm0s(x, c0, c1):
            rec = st[x]
            a = rec["sc0"][:, c0:c1]
            nc.scalar.activation(out=a, in_=a, func=ACT.Copy, scale=rec["rr"][:, 0:1])

        rowmin(z, 1)
        expo(z, 0)
        expo(z, 1)
        copy_group(z - 3, 0, "v")
        copy_group(z - 3, 1, "v")
        tc2(z - 3, 2, "s")
        tc2(z - 3, 3, "s")
        quant(z - 4)
        recip_map(z - 1, 0)
        recip_map(z - 1, 1)
        norm0(z - 1, 0, S)
        combine(z - 1, 0, HALF)
        tc2(z - 2, 0, "s", False)
        pv(z - 4)
        tc2(z - 2, 1, "s", False)
        combine(z - 1, HALF, S)
        recip_map(z, 0)
        norm0(z, 0, S)
        tb(z - 1, 0, "s")
        tb(z - 1, 1, "s")
        recip_map(z, 1)
        combine(z, 0, HALF)
        tc2(z - 2, 2, "s", False)
        tc2(z - 2, 3, "s", False)
        combine(z, HALF, S)
        finish2(z - 7, "s", "s")
        tb(z - 1, 2, "s")
        tb(z - 1, 3, "s")
        tb(z, 0, "s")
        tb(z, 1, "s")
        tb(z, 2, "s")
        tb(z, 3, "s")
        quant(z - 3)
        pv(z - 3)
        quant(z - 2)
        pv(z - 2)
        quant(z - 1)
        pv(z - 1, psc, "ps")
        stats(z - 5, 2)
        quant(z)
        pv(z, pat, "at", True)
        finish2(z - 5, "s", "s")
        stats(z - 3, 2)
        stats(z - 1, 2)
        finish2(z - 3, "v", "v")
        finish2(z - 1, "v", "s")
